import numpy as np
import ml_dtypes


def mxq(x, axis, fmt="e4m3"):
    dtype, down = {"e4m3": (ml_dtypes.float8_e4m3fn, 7), "e5m2": (ml_dtypes.float8_e5m2, 14)}[fmt]
    v = np.moveaxis(np.asarray(x, np.float32).astype(ml_dtypes.bfloat16).astype(np.float64), axis, -1)
    blocks = v.reshape(v.shape[:-1] + (-1, 32))
    amax = np.abs(blocks).max(-1, keepdims=True)
    byte = np.maximum(np.where(amax > 0, np.frexp(amax)[1] - 1 + 127, 0) - down, 1)
    scale = np.exp2(byte - 127.0)
    codes = (blocks / scale).astype(np.float32).astype(dtype).astype(np.float64)
    return np.moveaxis((codes * scale).reshape(v.shape), -1, axis)


WIDE = False


def mx_kscale(k):
    if not WIDE:
        return np.ones(k)
    levels = np.array([10, -10, 5, -5, 0])
    a = np.random.permutation(np.resize(levels, k // 512 * 4)).reshape(k // 512, 4)
    idx = np.arange(k)
    return np.exp2(a[idx // 512, idx % 128 // 32])


BF16 = ml_dtypes.bfloat16


def bf(x):
    return np.asarray(x, np.float32).astype(BF16)


def f64(x):
    return np.asarray(x).astype(np.float64)


E2M1 = np.array([0.0, 0.5, 1.0, 1.5, 2.0, 3.0, 4.0, 6.0, -0.0, -0.5, -1.0, -1.5, -2.0, -3.0, -4.0, -6.0])


def pack_weight(w, fmt):
    k, n = w.shape
    w = f64(bf(w)).reshape(k // 32, 32, n)
    amax = np.abs(w).max(1)
    if fmt == "e4m3":
        byte = np.frexp(amax)[1] - 1 + 127 - 7
    else:
        mant, ex = np.frexp(amax / 6.0)
        byte = np.where(mant > 0.5, ex, ex - 1) + 127
    byte = np.clip(np.where(amax > 0, byte, 1), 1, 254)
    scaled = (w * np.exp2(127.0 - byte)[:, None, :]).reshape(k, n).astype(np.float32)
    by_word = np.ascontiguousarray(scaled.reshape(k // 512, 128, 4, n).transpose(0, 1, 3, 2))
    if fmt == "e4m3":
        words = by_word.astype(ml_dtypes.float8_e4m3fn).view(np.uint8)
    else:
        c = by_word.astype(ml_dtypes.float4_e2m1fn).view(np.uint8) & 0xF
        words = c[..., 0::2] | (c[..., 1::2] << 4)
    return np.ascontiguousarray(words), np.ascontiguousarray(byte.astype(np.uint8).reshape(k // 512, 16, n))


def unpack_weight(words, scales, fmt):
    g, p, n, _ = words.shape
    if fmt == "e4m3":
        vals = np.ascontiguousarray(words).view(ml_dtypes.float8_e4m3fn).astype(np.float64)
    else:
        nib = np.empty((g, p, n, 4), np.uint8)
        nib[..., 0::2] = words & 0xF
        nib[..., 1::2] = words >> 4
        vals = E2M1[nib]
    vals = vals * np.repeat(np.exp2(scales.astype(np.float64) - 127.0), 8, axis=1)[..., None]
    return vals.transpose(0, 1, 3, 2).reshape(g * 512, n)


B, IN, H = 256, 8192, 1024


def sigmoid(v):
    return 1.0 / (1.0 + np.exp(-v))


def setup_inputs():
    s = mx_kscale(IN)
    g = np.random.standard_normal((H, IN + H)) / np.sqrt(IN + H)
    g[:, :IN] /= s
    x = bf(np.random.standard_normal((B, IN)) * s)
    h = bf(np.random.standard_normal((B, H)))
    tau = bf(np.random.standard_normal(H))
    w_in = np.random.standard_normal((H, IN)) / np.sqrt(IN) / s
    w_rec = np.random.standard_normal((H, H)) * 1.5 / np.sqrt(H)
    gate_b = bf(np.random.standard_normal(H) * 0.5)
    W_in_words, W_in_scales = pack_weight(np.ascontiguousarray(w_in.T), "e4m3")
    W_rec_words, W_rec_scales = pack_weight(np.ascontiguousarray(w_rec.T), "e4m3")
    gate_w_words, gate_w_scales = pack_weight(np.ascontiguousarray(g.T), "e4m3")
    return {"x": x,
            "h": h,
            "tau": tau,
            "W_in_words": W_in_words,
            "W_in_scales": W_in_scales,
            "W_rec_words": W_rec_words,
            "W_rec_scales": W_rec_scales,
            "gate_w_words": gate_w_words,
            "gate_w_scales": gate_w_scales,
            "gate_b": gate_b}


def reference(x, h, tau, W_in_words, W_in_scales, W_rec_words, W_rec_scales, gate_w_words, gate_w_scales, gate_b):
    tau_p = np.log(1.0 + np.exp(f64(tau))) + 1.0
    gt = unpack_weight(gate_w_words, gate_w_scales, "e4m3")
    xq = mxq(f64(x), 1, "e4m3")
    hq = mxq(f64(h), 1, "e4m3")
    x_in = xq @ unpack_weight(W_in_words, W_in_scales, "e4m3")
    pre = (xq @ gt[:IN]) + (hq @ gt[IN:]) + f64(gate_b)
    gate = sigmoid(np.tanh(pre))
    k1 = -f64(h) / tau_p + x_in + gate * (hq @ unpack_weight(W_rec_words, W_rec_scales, "e4m3"))
    return x_in, k1

@@ -1,0 +1,272 @@
+from contextlib import ExitStack
+
+import concourse.mybir as mybir
+from concourse.masks import make_identity
+
+F32 = mybir.dt.float32
+BF16 = mybir.dt.bfloat16
+I32 = mybir.dt.int32
+U32 = mybir.dt.uint32
+U8 = mybir.dt.uint8
+FP8X4 = mybir.dt.float8_e4m3fn_x4
+ALU = mybir.AluOpType
+ACT = mybir.ActivationFunctionType
+
+P = 128
+PACK = 4
+K_PASS = P * PACK
+B, IN, H = 256, 8192, 1024
+ROW_TILES = B // P
+N_TILE = 512
+COL_TILES = H // N_TILE
+X_GROUPS = IN // K_PASS
+H_GROUPS = H // K_PASS
+A_GROUPS = X_GROUPS + H_GROUPS
+CHUNK_GROUPS = 4
+X_CHUNKS = X_GROUPS // CHUNK_GROUPS
+A_CHUNKS = X_CHUNKS + 1
+CHUNKS_AHEAD = 2
+WORDS = K_PASS // 2
+PLANES_PER_BLOCK = 4
+QUADRANTS = 4
+W_BUFS = 16
+
+FLOPS = 2 * B * H * (IN + (IN + H) + H)
+
+
+def tile_ltccell_pa_k_kernel(
+    tc,
+    x,
+    h,
+    tau,
+    W_in_words,
+    W_in_scales,
+    W_rec_words,
+    W_rec_scales,
+    gate_w_words,
+    gate_w_scales,
+    gate_b,
+    out_0,
+    out_1,
+):
+    nc = tc.nc
+
+    GATE_SLOT = 0
+    REC_SLOT = GATE_SLOT + A_GROUPS
+    IN_SLOT = REC_SLOT + H_GROUPS
+    N_SLOTS = IN_SLOT + X_GROUPS
+    slot_words = []
+    scales_at = {}
+    for first_slot, words, scales in (
+        (GATE_SLOT, gate_w_words, gate_w_scales),
+        (REC_SLOT, W_rec_words, W_rec_scales),
+        (IN_SLOT, W_in_words, W_in_scales),
+    ):
+        groups = words.shape[0]
+        scales_at[first_slot] = (scales, groups)
+        for g in range(groups):
+            slot_words.append(words[g].rearrange("p n t -> p (n t)").bitcast(I32))
+    N_BLOCKS = N_SLOTS // PLANES_PER_BLOCK
+
+    with ExitStack() as ctx:
+        keep = ctx.enter_context(tc.tile_pool(name="keep", bufs=1))
+        raw_pool = ctx.enter_context(tc.tile_pool(name="raw", bufs=X_CHUNKS))
+        grouped_pool = ctx.enter_context(tc.tile_pool(name="grouped", bufs=2))
+        w_pool = ctx.enter_context(tc.tile_pool(name="w", bufs=W_BUFS))
+        gate_pool = ctx.enter_context(tc.tile_pool(name="gate", bufs=2))
+        out_pool = ctx.enter_context(tc.tile_pool(name="out", bufs=ROW_TILES * COL_TILES))
+        acc_pool = ctx.enter_context(tc.psum_pool(name="acc", bufs=1))
+        work_pool = ctx.enter_context(tc.psum_pool(name="work", bufs=CHUNK_GROUPS))
+        ctx.enter_context(tc.manual_schedule())
+
+        a_codes = keep.tile([P, A_GROUPS, B], U32, align_bytes=64)
+        a_planes = keep.tile([P, A_GROUPS, B], U8, align_bytes=64)
+        w_planes = keep.tile([P, N_BLOCKS, H], U8, align_bytes=64)
+        h_raw = keep.tile([P, ROW_TILES, H], BF16)
+        identity = keep.tile([P, P], F32)
+        ones = keep.tile([P, P], BF16)
+        vec_rows = keep.tile([P, 2, H], BF16)
+        tau_sb = keep.tile([P, H], F32)
+        bias_sb = keep.tile([P, H], F32)
+        base = keep.tile([P, ROW_TILES, H], F32)
+        half_rec = keep.tile([P, ROW_TILES, H], F32)
+
+        nc.vector.memset(vec_rows[:], 0.0)
+        nc.vector.memset(ones[:], 1.0)
+        nc.vector.memset(w_planes[:].rearrange("p c n -> p (c n)").bitcast(I32), 0)
+        make_identity(nc, identity[:])
+
+        raw_tiles = {}
+        w_tiles = {}
+
+        def load_raw(chunk):
+            if chunk < X_CHUNKS:
+                raw = raw_pool.tile([P, ROW_TILES, CHUNK_GROUPS * K_PASS], BF16)
+                k_cols = slice(chunk * CHUNK_GROUPS * K_PASS, (chunk + 1) * CHUNK_GROUPS * K_PASS)
+                nc.sync.dma_start(out=raw[:], in_=x[:, k_cols].rearrange("(m p) k -> p m k", p=P))
+                raw_tiles[chunk] = raw
+            elif chunk < A_CHUNKS:
+                nc.sync.dma_start(out=h_raw[:], in_=h.rearrange("(m p) k -> p m k", p=P))
+                raw_tiles[chunk] = h_raw
+
+        def load_planes(first_slot):
+            scales, groups = scales_at[first_slot]
+            end_slot = first_slot + groups
+            for block in range(first_slot // PLANES_PER_BLOCK, (end_slot - 1) // PLANES_PER_BLOCK + 1):
+                lo = max(first_slot, block * PLANES_PER_BLOCK)
+                hi = min(end_slot, (block + 1) * PLANES_PER_BLOCK)
+                for quad in range(QUADRANTS):
+                    row = 32 * quad + 4 * (lo % PLANES_PER_BLOCK)
+                    nc.sync.dma_start(
+                        out=w_planes[row : row + 4 * (hi - lo), block, :].bitcast(I32),
+                        in_=scales[lo - first_slot : hi - first_slot, 4 * quad : 4 * quad + 4, :].bitcast(I32),
+                    )
+
+        def fetch(slot):
+            if slot < N_SLOTS:
+                if slot in scales_at:
+                    load_planes(slot)
+                w = w_pool.tile([P, H], I32, align_bytes=64)
+                nc.sync.dma_start(out=w[:], in_=slot_words[slot])
+                w_tiles[slot] = w
+
+        def prepare(chunk):
+            raw = raw_tiles[chunk]
+            groups = raw.shape[2] // K_PASS
+            grouped = grouped_pool.tile([P, CHUNK_GROUPS, B * PACK], BF16, align_bytes=64)
+            for gi in range(groups):
+                flipped = work_pool.tile([P, 2, B], F32, tag="work")
+                for m in range(ROW_TILES):
+                    words = raw[:, m, :].bitcast(F32)
+                    for u in range(2):
+                        nc.tensor.transpose(
+                            flipped[:, u, m * P : (m + 1) * P],
+                            words[:, gi * WORDS + u : (gi + 1) * WORDS : 2],
+                            identity[:],
+                        )
+                copy_out = nc.vector.tensor_copy if gi % 2 == 0 else nc.scalar.copy
+                copy_out(
+                    out=grouped[:, gi, :].bitcast(F32).rearrange("p (b u) -> p b u", u=2),
+                    in_=flipped[:].rearrange("p u b -> p b u"),
+                )
+            first = chunk * CHUNK_GROUPS
+            nc.vector.quantize_mx(
+                out=a_codes[:, first : first + groups, :].rearrange("p g b -> p (g b)").bitcast(FP8X4),
+                scales=a_planes[:, first : first + groups, :].rearrange("p g b -> p (g b)"),
+                in_=grouped[:, 0:groups, :].rearrange("p g e -> p (g e)"),
+            )
+
+        def new_banks(label):
+            return [
+                [
+                    acc_pool.tile([P, N_TILE], F32, name="%s%d%d" % (label, m, n), tag="acc%d%d" % (m, n))
+                    for n in range(COL_TILES)
+                ]
+                for m in range(ROW_TILES)
+            ]
+
+        def mx_passes(banks, slot, a_group, start, stop):
+            block = slot // PLANES_PER_BLOCK
+            row = 4 * (slot % PLANES_PER_BLOCK)
+            for m in range(ROW_TILES):
+                b_cols = slice(m * P, (m + 1) * P)
+                for n in range(COL_TILES):
+                    n_cols = slice(n * N_TILE, (n + 1) * N_TILE)
+                    nc.tensor.matmul_mx(
+                        out=banks[m][n][:],
+                        lhsT=a_codes[:, a_group, b_cols].bitcast(FP8X4),
+                        lhsT_scale=a_planes[:, a_group, b_cols],
+                        rhs=w_tiles[slot][:, n_cols].bitcast(FP8X4),
+                        rhs_scale=w_planes[row:P, block, n_cols],
+                        start=start,
+                        stop=stop,
+                    )
+
+        nc.scalar.dma_start(out=vec_rows[0:1, 0, :], in_=tau.unsqueeze(0))
+        nc.scalar.dma_start(out=vec_rows[0:1, 1, :], in_=gate_b.unsqueeze(0))
+        for chunk in range(CHUNKS_AHEAD):
+            load_raw(chunk)
+        for chunk in range(W_BUFS // CHUNK_GROUPS):
+            for slot in range(chunk * CHUNK_GROUPS, (chunk + 1) * CHUNK_GROUPS):
+                fetch(slot)
+            load_raw(chunk + CHUNKS_AHEAD)
+
+        for v, spread in enumerate((tau_sb, bias_sb)):
+            for n in range(COL_TILES):
+                n_cols = slice(n * N_TILE, (n + 1) * N_TILE)
+                repeated = work_pool.tile([P, N_TILE], F32, tag="work")
+                nc.tensor.matmul(out=repeated[:], lhsT=ones[:], rhs=vec_rows[:, v, n_cols], start=True, stop=True)
+                nc.scalar.copy(out=spread[:, n_cols], in_=repeated[:])
+
+        for chunk in range(CHUNKS_AHEAD):
+            prepare(chunk)
+        pre = new_banks("pre")
+        for g in range(A_GROUPS):
+            mx_passes(pre, GATE_SLOT + g, g, start=(g == 0), stop=(g == A_GROUPS - 1))
+            fetch(GATE_SLOT + g + W_BUFS)
+            next_chunk = g // CHUNK_GROUPS + CHUNKS_AHEAD
+            if g % CHUNK_GROUPS == CHUNK_GROUPS - 1 and next_chunk < A_CHUNKS:
+                prepare(next_chunk)
+
+        soft = keep.tile([P, H], F32)
+        nc.vector.scalar_tensor_tensor(
+            out=soft[:], in0=tau_sb[:], scalar=-1.0, in1=tau_sb[:], op0=ALU.mult, op1=ALU.min
+        )
+        nc.scalar.activation(out=soft[:], in_=soft[:], func=ACT.Exp)
+        nc.scalar.activation(out=soft[:], in_=soft[:], func=ACT.Ln, bias=1.0)
+        tau_p = keep.tile([P, H], F32)
+        nc.vector.tensor_scalar(out=tau_p[:], in0=tau_sb[:], scalar1=0.0, scalar2=1.0, op0=ALU.max, op1=ALU.add)
+        nc.vector.tensor_tensor(out=tau_p[:], in0=tau_p[:], in1=soft[:], op=ALU.add)
+        inv_tau_p = keep.tile([P, H], F32)
+        nc.vector.reciprocal(out=inv_tau_p[:], in_=tau_p[:])
+        for m in range(ROW_TILES):
+            nc.vector.scalar_tensor_tensor(
+                out=base[:, m, :], in0=h_raw[:, m, :], scalar=-1.0, in1=inv_tau_p[:], op0=ALU.mult, op1=ALU.mult
+            )
+
+        tiles = [(m, n) for m in range(ROW_TILES) for n in range(COL_TILES)]
+        pre_b = {}
+        for m, n in tiles:
+            biased = gate_pool.tile([P, N_TILE], F32, bufs=len(tiles))
+            nc.vector.tensor_tensor(
+                out=biased[:], in0=pre[m][n][:], in1=bias_sb[:, n * N_TILE : (n + 1) * N_TILE], op=ALU.add
+            )
+            pre_b[(m, n)] = biased
+
+        rec = [
+            [work_pool.tile([P, N_TILE], F32, name="rec%d%d" % (m, n), tag="work") for n in range(COL_TILES)]
+            for m in range(ROW_TILES)
+        ]
+        for g in range(H_GROUPS):
+            mx_passes(rec, REC_SLOT + g, X_GROUPS + g, start=(g == 0), stop=(g == H_GROUPS - 1))
+            fetch(REC_SLOT + g + W_BUFS)
+
+        for m, n in tiles:
+            n_cols = slice(n * N_TILE, (n + 1) * N_TILE)
+            nc.scalar.activation(out=half_rec[:, m, n_cols], in_=rec[m][n][:], func=ACT.Copy, scale=0.5)
+        for m, n in tiles:
+            n_cols = slice(n * N_TILE, (n + 1) * N_TILE)
+            inner = gate_pool.tile([P, N_TILE], F32)
+            nc.scalar.activation(out=inner[:], in_=pre_b[(m, n)][:], func=ACT.Tanh)
+            outer = gate_pool.tile([P, N_TILE], F32)
+            nc.scalar.activation(out=outer[:], in_=inner[:], func=ACT.Tanh, scale=0.5)
+            gated = gate_pool.tile([P, N_TILE], F32)
+            nc.vector.scalar_tensor_tensor(
+                out=gated[:], in0=outer[:], scalar=1.0, in1=half_rec[:, m, n_cols], op0=ALU.add, op1=ALU.mult
+            )
+            nc.vector.tensor_tensor(out=base[:, m, n_cols], in0=base[:, m, n_cols], in1=gated[:], op=ALU.add)
+
+        x_in = new_banks("x_in")
+        for g in range(X_GROUPS):
+            mx_passes(x_in, IN_SLOT + g, g, start=(g == 0), stop=(g == X_GROUPS - 1))
+            fetch(IN_SLOT + g + W_BUFS)
+
+        for m, n in tiles:
+            b_rows = slice(m * P, (m + 1) * P)
+            n_cols = slice(n * N_TILE, (n + 1) * N_TILE)
+            x_in_sb = out_pool.tile([P, N_TILE], F32)
+            nc.scalar.copy(out=x_in_sb[:], in_=x_in[m][n][:])
+            nc.sync.dma_start(out=out_0[b_rows, n_cols], in_=x_in_sb[:])
+            k1_sb = out_pool.tile([P, N_TILE], F32)
+            nc.vector.tensor_tensor(out=k1_sb[:], in0=x_in_sb[:], in1=base[:, m, n_cols], op=ALU.add)
+            nc.sync.dma_start(out=out_1[b_rows, n_cols], in_=k1_sb[:])

@@ -117,15 +117,13 @@ def tile_ltccell_pa_k_kernel(
                 hi = min(end_slot, (block + 1) * PLANES_PER_BLOCK)
                 for quad in range(QUADRANTS):
                     row = 32 * quad + 4 * (lo % PLANES_PER_BLOCK)
-                    nc.sync.dma_start(
-                        out=w_planes[row : row + 4 * (hi - lo), block, :].bitcast(I32),
-                        in_=scales[lo - first_slot : hi - first_slot, 4 * quad : 4 * quad + 4, :].bitcast(I32),
+                    nc.gpsimd.dma_start(
+                        out=w_planes[row : row + 4 * (hi - lo), block, :].bitcast(F32),
+                        in_=scales[lo - first_slot : hi - first_slot, 4 * quad : 4 * quad + 4, :].bitcast(F32),
                     )
 
         def fetch(slot):
             if slot < N_SLOTS:
-                if slot in scales_at:
-                    load_planes(slot)
                 w = w_pool.tile([P, H], I32, align_bytes=64)
                 nc.sync.dma_start(out=w[:], in_=slot_words[slot])
                 w_tiles[slot] = w
@@ -184,6 +182,8 @@ def tile_ltccell_pa_k_kernel(
 
         nc.scalar.dma_start(out=vec_rows[0:1, 0, :], in_=tau.unsqueeze(0))
         nc.scalar.dma_start(out=vec_rows[0:1, 1, :], in_=gate_b.unsqueeze(0))
+        for first_slot in (GATE_SLOT, REC_SLOT, IN_SLOT):
+            load_planes(first_slot)
         for chunk in range(CHUNKS_AHEAD):
             load_raw(chunk)
         for chunk in range(W_BUFS // CHUNK_GROUPS):

@@ -26,10 +26,9 @@ CHUNK_GROUPS = 4
 X_CHUNKS = X_GROUPS // CHUNK_GROUPS
 A_CHUNKS = X_CHUNKS + 1
 CHUNKS_AHEAD = 2
-WORDS = K_PASS // 2
 PLANES_PER_BLOCK = 4
 QUADRANTS = 4
-W_BUFS = 16
+W_BUFS = 12
 
 FLOPS = 2 * B * H * (IN + (IN + H) + H)
 
@@ -71,6 +70,7 @@ def tile_ltccell_pa_k_kernel(
     with ExitStack() as ctx:
         keep = ctx.enter_context(tc.tile_pool(name="keep", bufs=1))
         raw_pool = ctx.enter_context(tc.tile_pool(name="raw", bufs=X_CHUNKS))
+        ordered_pool = ctx.enter_context(tc.tile_pool(name="ordered", bufs=2))
         grouped_pool = ctx.enter_context(tc.tile_pool(name="grouped", bufs=2))
         w_pool = ctx.enter_context(tc.tile_pool(name="w", bufs=W_BUFS))
         gate_pool = ctx.enter_context(tc.tile_pool(name="gate", bufs=2))
@@ -91,9 +91,9 @@ def tile_ltccell_pa_k_kernel(
         base = keep.tile([P, ROW_TILES, H], F32)
         half_rec = keep.tile([P, ROW_TILES, H], F32)
 
-        nc.vector.memset(vec_rows[:], 0.0)
-        nc.vector.memset(ones[:], 1.0)
         nc.vector.memset(w_planes[:].rearrange("p c n -> p (c n)").bitcast(I32), 0)
+        nc.vector.memset(vec_rows[:].rearrange("p v n -> p (v n)").bitcast(I32), 0)
+        nc.vector.memset(ones[:], 1.0)
         make_identity(nc, identity[:])
 
         raw_tiles = {}
@@ -131,17 +131,19 @@ def tile_ltccell_pa_k_kernel(
         def prepare(chunk):
             raw = raw_tiles[chunk]
             groups = raw.shape[2] // K_PASS
+            ordered = ordered_pool.tile([P, ROW_TILES, CHUNK_GROUPS, 2, P], F32)
+            for m in range(ROW_TILES):
+                copy_words = nc.vector.tensor_copy if m % 2 == 0 else nc.scalar.copy
+                copy_words(
+                    out=ordered[:, m, 0:groups, :, :],
+                    in_=raw[:, m, :].bitcast(F32).rearrange("p (g q u) -> p g u q", q=P, u=2),
+                )
             grouped = grouped_pool.tile([P, CHUNK_GROUPS, B * PACK], BF16, align_bytes=64)
             for gi in range(groups):
                 flipped = work_pool.tile([P, 2, B], F32, tag="work")
                 for m in range(ROW_TILES):
-                    words = raw[:, m, :].bitcast(F32)
                     for u in range(2):
-                        nc.tensor.transpose(
-                            flipped[:, u, m * P : (m + 1) * P],
-                            words[:, gi * WORDS + u : (gi + 1) * WORDS : 2],
-                            identity[:],
-                        )
+                        nc.tensor.transpose(flipped[:, u, m * P : (m + 1) * P], ordered[:, m, gi, u, :], identity[:])
                 copy_out = nc.vector.tensor_copy if gi % 2 == 0 else nc.scalar.copy
                 copy_out(
                     out=grouped[:, gi, :].bitcast(F32).rearrange("p (b u) -> p b u", u=2),
@@ -191,38 +193,32 @@ def tile_ltccell_pa_k_kernel(
                 fetch(slot)
             load_raw(chunk + CHUNKS_AHEAD)
 
-        for v, spread in enumerate((tau_sb, bias_sb)):
-            for n in range(COL_TILES):
-                n_cols = slice(n * N_TILE, (n + 1) * N_TILE)
-                repeated = work_pool.tile([P, N_TILE], F32, tag="work")
-                nc.tensor.matmul(out=repeated[:], lhsT=ones[:], rhs=vec_rows[:, v, n_cols], start=True, stop=True)
-                nc.scalar.copy(out=spread[:, n_cols], in_=repeated[:])
-
         for chunk in range(CHUNKS_AHEAD):
             prepare(chunk)
+
         pre = new_banks("pre")
-        for g in range(A_GROUPS):
-            mx_passes(pre, GATE_SLOT + g, g, start=(g == 0), stop=(g == A_GROUPS - 1))
+        for g in range(X_GROUPS):
+            mx_passes(pre, GATE_SLOT + g, g, start=(g == 0), stop=False)
             fetch(GATE_SLOT + g + W_BUFS)
             next_chunk = g // CHUNK_GROUPS + CHUNKS_AHEAD
             if g % CHUNK_GROUPS == CHUNK_GROUPS - 1 and next_chunk < A_CHUNKS:
                 prepare(next_chunk)
 
+        for v, (spread, copy_out) in enumerate(((tau_sb, nc.scalar.copy), (bias_sb, nc.vector.tensor_copy))):
+            for n in range(COL_TILES):
+                n_cols = slice(n * N_TILE, (n + 1) * N_TILE)
+                repeated = work_pool.tile([P, N_TILE], F32, tag="work")
+                nc.tensor.matmul(out=repeated[:], lhsT=ones[:], rhs=vec_rows[:, v, n_cols], start=True, stop=True)
+                copy_out(out=spread[:, n_cols], in_=repeated[:])
+
+        for g in range(X_GROUPS, A_GROUPS):
+            mx_passes(pre, GATE_SLOT + g, g, start=False, stop=(g == A_GROUPS - 1))
+            fetch(GATE_SLOT + g + W_BUFS)
+
         soft = keep.tile([P, H], F32)
-        nc.vector.scalar_tensor_tensor(
-            out=soft[:], in0=tau_sb[:], scalar=-1.0, in1=tau_sb[:], op0=ALU.mult, op1=ALU.min
-        )
-        nc.scalar.activation(out=soft[:], in_=soft[:], func=ACT.Exp)
+        nc.scalar.activation(out=soft[:], in_=tau_sb[:], func=ACT.Abs)
+        nc.scalar.activation(out=soft[:], in_=soft[:], func=ACT.Exp, scale=-1.0)
         nc.scalar.activation(out=soft[:], in_=soft[:], func=ACT.Ln, bias=1.0)
-        tau_p = keep.tile([P, H], F32)
-        nc.vector.tensor_scalar(out=tau_p[:], in0=tau_sb[:], scalar1=0.0, scalar2=1.0, op0=ALU.max, op1=ALU.add)
-        nc.vector.tensor_tensor(out=tau_p[:], in0=tau_p[:], in1=soft[:], op=ALU.add)
-        inv_tau_p = keep.tile([P, H], F32)
-        nc.vector.reciprocal(out=inv_tau_p[:], in_=tau_p[:])
-        for m in range(ROW_TILES):
-            nc.vector.scalar_tensor_tensor(
-                out=base[:, m, :], in0=h_raw[:, m, :], scalar=-1.0, in1=inv_tau_p[:], op0=ALU.mult, op1=ALU.mult
-            )
 
         tiles = [(m, n) for m in range(ROW_TILES) for n in range(COL_TILES)]
         pre_b = {}
@@ -244,6 +240,19 @@ def tile_ltccell_pa_k_kernel(
         for m, n in tiles:
             n_cols = slice(n * N_TILE, (n + 1) * N_TILE)
             nc.scalar.activation(out=half_rec[:, m, n_cols], in_=rec[m][n][:], func=ACT.Copy, scale=0.5)
+
+        softplus = keep.tile([P, H], F32)
+        nc.vector.scalar_tensor_tensor(
+            out=softplus[:], in0=tau_sb[:], scalar=0.0, in1=soft[:], op0=ALU.max, op1=ALU.add
+        )
+        inv_tau_p = keep.tile([P, H], F32)
+        nc.scalar.activation(out=inv_tau_p[:], in_=softplus[:], func=ACT.Ln, bias=1.0)
+        nc.scalar.activation(out=inv_tau_p[:], in_=inv_tau_p[:], func=ACT.Exp, scale=-1.0)
+        for m in range(ROW_TILES):
+            nc.vector.scalar_tensor_tensor(
+                out=base[:, m, :], in0=h_raw[:, m, :], scalar=-1.0, in1=inv_tau_p[:], op0=ALU.mult, op1=ALU.mult
+            )
+
         for m, n in tiles:
             n_cols = slice(n * N_TILE, (n + 1) * N_TILE)
             inner = gate_pool.tile([P, N_TILE], F32)

@@ -29,6 +29,7 @@ CHUNKS_AHEAD = 2
 PLANES_PER_BLOCK = 4
 QUADRANTS = 4
 W_BUFS = 12
+TAPER_GROUPS = 4
 
 FLOPS = 2 * B * H * (IN + (IN + H) + H)
 
@@ -66,6 +67,9 @@ def tile_ltccell_pa_k_kernel(
         for g in range(groups):
             slot_words.append(words[g].rearrange("p n t -> p (n t)").bitcast(I32))
     N_BLOCKS = N_SLOTS // PLANES_PER_BLOCK
+    pieces = [(slot, 0, COL_TILES) for slot in range(N_SLOTS - TAPER_GROUPS)]
+    for n in range(COL_TILES):
+        pieces.extend([(slot, n, 1) for slot in range(N_SLOTS - TAPER_GROUPS, N_SLOTS)])
 
     with ExitStack() as ctx:
         keep = ctx.enter_context(tc.tile_pool(name="keep", bufs=1))
@@ -122,11 +126,12 @@ def tile_ltccell_pa_k_kernel(
                         in_=scales[lo - first_slot : hi - first_slot, 4 * quad : 4 * quad + 4, :].bitcast(F32),
                     )
 
-        def fetch(slot):
-            if slot < N_SLOTS:
-                w = w_pool.tile([P, H], I32, align_bytes=64)
-                nc.sync.dma_start(out=w[:], in_=slot_words[slot])
-                w_tiles[slot] = w
+        def fetch(piece):
+            if piece < len(pieces):
+                slot, first_n, count = pieces[piece]
+                w = w_pool.tile([P, count * N_TILE], I32, align_bytes=64)
+                nc.sync.dma_start(out=w[:], in_=slot_words[slot][:, first_n * N_TILE : (first_n + count) * N_TILE])
+                w_tiles[piece] = w
 
         def prepare(chunk):
             raw = raw_tiles[chunk]
@@ -165,19 +170,20 @@ def tile_ltccell_pa_k_kernel(
                 for m in range(ROW_TILES)
             ]
 
-        def mx_passes(banks, slot, a_group, start, stop):
+        def mx_passes(banks, piece, a_group, start, stop):
+            slot, first_n, count = pieces[piece]
             block = slot // PLANES_PER_BLOCK
             row = 4 * (slot % PLANES_PER_BLOCK)
             for m in range(ROW_TILES):
                 b_cols = slice(m * P, (m + 1) * P)
-                for n in range(COL_TILES):
-                    n_cols = slice(n * N_TILE, (n + 1) * N_TILE)
+                for i in range(count):
+                    n = first_n + i
                     nc.tensor.matmul_mx(
                         out=banks[m][n][:],
                         lhsT=a_codes[:, a_group, b_cols].bitcast(FP8X4),
                         lhsT_scale=a_planes[:, a_group, b_cols],
-                        rhs=w_tiles[slot][:, n_cols].bitcast(FP8X4),
-                        rhs_scale=w_planes[row:P, block, n_cols],
+                        rhs=w_tiles[piece][:, i * N_TILE : (i + 1) * N_TILE].bitcast(FP8X4),
+                        rhs_scale=w_planes[row:P, block, n * N_TILE : (n + 1) * N_TILE],
                         start=start,
                         stop=stop,
                     )
@@ -265,12 +271,7 @@ def tile_ltccell_pa_k_kernel(
             )
             nc.vector.tensor_tensor(out=base[:, m, n_cols], in0=base[:, m, n_cols], in1=gated[:], op=ALU.add)
 
-        x_in = new_banks("x_in")
-        for g in range(X_GROUPS):
-            mx_passes(x_in, IN_SLOT + g, g, start=(g == 0), stop=(g == X_GROUPS - 1))
-            fetch(IN_SLOT + g + W_BUFS)
-
-        for m, n in tiles:
+        def write_out(m, n):
             b_rows = slice(m * P, (m + 1) * P)
             n_cols = slice(n * N_TILE, (n + 1) * N_TILE)
             x_in_sb = out_pool.tile([P, N_TILE], F32)
@@ -279,3 +280,14 @@ def tile_ltccell_pa_k_kernel(
             k1_sb = out_pool.tile([P, N_TILE], F32)
             nc.vector.tensor_tensor(out=k1_sb[:], in0=x_in_sb[:], in1=base[:, m, n_cols], op=ALU.add)
             nc.sync.dma_start(out=out_1[b_rows, n_cols], in_=k1_sb[:])
+
+        x_in = new_banks("x_in")
+        for piece in range(IN_SLOT, len(pieces)):
+            slot, first_n, count = pieces[piece]
+            g = slot - IN_SLOT
+            mx_passes(x_in, piece, g, start=(g == 0), stop=(g == X_GROUPS - 1))
+            fetch(piece + W_BUFS)
+            if g == X_GROUPS - 1:
+                for n in range(first_n, first_n + count):
+                    for m in range(ROW_TILES):
+                        write_out(m, n)

@@ -95,6 +95,9 @@ def tile_ltccell_pa_k_kernel(
         base = keep.tile([P, ROW_TILES, H], F32)
         half_rec = keep.tile([P, ROW_TILES, H], F32)
 
+        warm = keep.tile([P, 2], F32)
+        nc.vector.memset(warm[:, 0:1], 0.0)
+        nc.scalar.copy(out=warm[:, 1:2], in_=warm[:, 0:1])
         nc.vector.memset(w_planes[:].rearrange("p c n -> p (c n)").bitcast(I32), 0)
         nc.vector.memset(vec_rows[:].rearrange("p v n -> p (v n)").bitcast(I32), 0)
         nc.vector.memset(ones[:], 1.0)
@@ -133,7 +136,10 @@ def tile_ltccell_pa_k_kernel(
                 nc.sync.dma_start(out=w[:], in_=slot_words[slot][:, first_n * N_TILE : (first_n + count) * N_TILE])
                 w_tiles[piece] = w
 
-        def prepare(chunk):
+        ordered_tiles = {}
+        grouped_tiles = {}
+
+        def sort_words(chunk):
             raw = raw_tiles[chunk]
             groups = raw.shape[2] // K_PASS
             ordered = ordered_pool.tile([P, ROW_TILES, CHUNK_GROUPS, 2, P], F32)
@@ -143,6 +149,11 @@ def tile_ltccell_pa_k_kernel(
                     out=ordered[:, m, 0:groups, :, :],
                     in_=raw[:, m, :].bitcast(F32).rearrange("p (g q u) -> p g u q", q=P, u=2),
                 )
+            ordered_tiles[chunk] = ordered
+
+        def flip(chunk):
+            ordered = ordered_tiles[chunk]
+            groups = raw_tiles[chunk].shape[2] // K_PASS
             grouped = grouped_pool.tile([P, CHUNK_GROUPS, B * PACK], BF16, align_bytes=64)
             for gi in range(groups):
                 flipped = work_pool.tile([P, 2, B], F32, tag="work")
@@ -154,11 +165,14 @@ def tile_ltccell_pa_k_kernel(
                     out=grouped[:, gi, :].bitcast(F32).rearrange("p (b u) -> p b u", u=2),
                     in_=flipped[:].rearrange("p u b -> p b u"),
                 )
-            first = chunk * CHUNK_GROUPS
+            grouped_tiles[chunk] = grouped
+
+        def quantize(chunk, first_gi, count):
+            first = chunk * CHUNK_GROUPS + first_gi
             nc.vector.quantize_mx(
-                out=a_codes[:, first : first + groups, :].rearrange("p g b -> p (g b)").bitcast(FP8X4),
-                scales=a_planes[:, first : first + groups, :].rearrange("p g b -> p (g b)"),
-                in_=grouped[:, 0:groups, :].rearrange("p g e -> p (g e)"),
+                out=a_codes[:, first : first + count, :].rearrange("p g b -> p (g b)").bitcast(FP8X4),
+                scales=a_planes[:, first : first + count, :].rearrange("p g b -> p (g b)"),
+                in_=grouped_tiles[chunk][:, first_gi : first_gi + count, :].rearrange("p g e -> p (g e)"),
             )
 
         def new_banks(label):
@@ -192,23 +206,29 @@ def tile_ltccell_pa_k_kernel(
         nc.scalar.dma_start(out=vec_rows[0:1, 1, :], in_=gate_b.unsqueeze(0))
         for first_slot in (GATE_SLOT, REC_SLOT, IN_SLOT):
             load_planes(first_slot)
-        for chunk in range(CHUNKS_AHEAD):
+        for chunk in range(A_CHUNKS):
             load_raw(chunk)
-        for chunk in range(W_BUFS // CHUNK_GROUPS):
-            for slot in range(chunk * CHUNK_GROUPS, (chunk + 1) * CHUNK_GROUPS):
-                fetch(slot)
-            load_raw(chunk + CHUNKS_AHEAD)
+            fetch(2 * chunk)
+            fetch(2 * chunk + 1)
+        for slot in range(2 * A_CHUNKS, W_BUFS):
+            fetch(slot)
 
-        for chunk in range(CHUNKS_AHEAD):
-            prepare(chunk)
+        sort_words(0)
+        flip(0)
+        quantize(0, 0, 2)
+        quantize(0, 2, 2)
+        sort_words(1)
 
         pre = new_banks("pre")
         for g in range(X_GROUPS):
             mx_passes(pre, GATE_SLOT + g, g, start=(g == 0), stop=False)
             fetch(GATE_SLOT + g + W_BUFS)
-            next_chunk = g // CHUNK_GROUPS + CHUNKS_AHEAD
-            if g % CHUNK_GROUPS == CHUNK_GROUPS - 1 and next_chunk < A_CHUNKS:
-                prepare(next_chunk)
+            next_chunk = (g + 1) // 2
+            if g % 2 == 1 and next_chunk < A_CHUNKS:
+                flip(next_chunk)
+                quantize(next_chunk, 0, raw_tiles[next_chunk].shape[2] // K_PASS)
+                if next_chunk + 1 < A_CHUNKS:
+                    sort_words(next_chunk + 1)
 
         for v, (spread, copy_out) in enumerate(((tau_sb, nc.scalar.copy), (bias_sb, nc.vector.tensor_copy))):
             for n in range(COL_TILES):

@@ -116,18 +116,34 @@ def tile_ltccell_pa_k_kernel(
                 nc.sync.dma_start(out=h_raw[:], in_=h.rearrange("(m p) k -> p m k", p=P))
                 raw_tiles[chunk] = h_raw
 
-        def load_planes(first_slot):
+        def plane_loads(first_slot):
             scales, groups = scales_at[first_slot]
             end_slot = first_slot + groups
+            found = []
             for block in range(first_slot // PLANES_PER_BLOCK, (end_slot - 1) // PLANES_PER_BLOCK + 1):
                 lo = max(first_slot, block * PLANES_PER_BLOCK)
                 hi = min(end_slot, (block + 1) * PLANES_PER_BLOCK)
                 for quad in range(QUADRANTS):
                     row = 32 * quad + 4 * (lo % PLANES_PER_BLOCK)
-                    nc.gpsimd.dma_start(
-                        out=w_planes[row : row + 4 * (hi - lo), block, :].bitcast(F32),
-                        in_=scales[lo - first_slot : hi - first_slot, 4 * quad : 4 * quad + 4, :].bitcast(F32),
+                    found.append(
+                        (
+                            w_planes[row : row + 4 * (hi - lo), block, :],
+                            scales[lo - first_slot : hi - first_slot, 4 * quad : 4 * quad + 4, :],
+                        )
                     )
+            return found
+
+        all_planes = plane_loads(GATE_SLOT) + plane_loads(REC_SLOT) + plane_loads(IN_SLOT)
+        pool_planes = [pair for i, pair in enumerate(all_planes) if i % QUADRANTS < 2]
+        sync_planes = [pair for i, pair in enumerate(all_planes) if i % QUADRANTS >= 2]
+
+        woven = [0]
+
+        def weave():
+            if woven[0] < len(sync_planes):
+                plane_out, plane_in = sync_planes[woven[0]]
+                nc.sync.dma_start(out=plane_out.bitcast(I32), in_=plane_in.bitcast(I32))
+                woven[0] += 1
 
         def fetch(piece):
             if piece < len(pieces):
@@ -135,6 +151,7 @@ def tile_ltccell_pa_k_kernel(
                 w = w_pool.tile([P, count * N_TILE], I32, align_bytes=64)
                 nc.sync.dma_start(out=w[:], in_=slot_words[slot][:, first_n * N_TILE : (first_n + count) * N_TILE])
                 w_tiles[piece] = w
+                weave()
 
         ordered_tiles = {}
         grouped_tiles = {}
@@ -204,10 +221,13 @@ def tile_ltccell_pa_k_kernel(
 
         nc.scalar.dma_start(out=vec_rows[0:1, 0, :], in_=tau.unsqueeze(0))
         nc.scalar.dma_start(out=vec_rows[0:1, 1, :], in_=gate_b.unsqueeze(0))
-        for first_slot in (GATE_SLOT, REC_SLOT, IN_SLOT):
-            load_planes(first_slot)
+        for plane_out, plane_in in pool_planes:
+            nc.gpsimd.dma_start(out=plane_out.bitcast(F32), in_=plane_in.bitcast(F32))
         for chunk in range(A_CHUNKS):
             load_raw(chunk)
+            if chunk == 0:
+                weave()
+                weave()
             fetch(2 * chunk)
             fetch(2 * chunk + 1)
         for slot in range(2 * A_CHUNKS, W_BUFS):

@@ -85,8 +85,8 @@ def tile_ltccell_pa_k_kernel(
 
         a_codes = keep.tile([P, A_GROUPS, B], U32, align_bytes=64)
         a_planes = keep.tile([P, A_GROUPS, B], U8, align_bytes=64)
-        w_planes = keep.tile([P, N_BLOCKS, H], U8, align_bytes=64)
-        h_raw = keep.tile([P, ROW_TILES, H], BF16)
+        w_planes = keep.tile([P, N_BLOCKS, H], U8, align_bytes=256)
+        h_raw = keep.tile([P, ROW_TILES, H], BF16, align_bytes=256)
         identity = keep.tile([P, P], F32)
         ones = keep.tile([P, P], BF16)
         vec_rows = keep.tile([P, 2, H], BF16)
@@ -108,7 +108,7 @@ def tile_ltccell_pa_k_kernel(
 
         def load_raw(chunk):
             if chunk < X_CHUNKS:
-                raw = raw_pool.tile([P, ROW_TILES, CHUNK_GROUPS * K_PASS], BF16)
+                raw = raw_pool.tile([P, ROW_TILES, CHUNK_GROUPS * K_PASS], BF16, align_bytes=256)
                 k_cols = slice(chunk * CHUNK_GROUPS * K_PASS, (chunk + 1) * CHUNK_GROUPS * K_PASS)
                 nc.sync.dma_start(out=raw[:], in_=x[:, k_cols].rearrange("(m p) k -> p m k", p=P))
                 raw_tiles[chunk] = raw
@@ -148,7 +148,7 @@ def tile_ltccell_pa_k_kernel(
         def fetch(piece):
             if piece < len(pieces):
                 slot, first_n, count = pieces[piece]
-                w = w_pool.tile([P, count * N_TILE], I32, align_bytes=64)
+                w = w_pool.tile([P, count * N_TILE], I32, align_bytes=256)
                 nc.sync.dma_start(out=w[:], in_=slot_words[slot][:, first_n * N_TILE : (first_n + count) * N_TILE])
                 w_tiles[piece] = w
                 weave()
@@ -314,10 +314,10 @@ def tile_ltccell_pa_k_kernel(
         def write_out(m, n):
             b_rows = slice(m * P, (m + 1) * P)
             n_cols = slice(n * N_TILE, (n + 1) * N_TILE)
-            x_in_sb = out_pool.tile([P, N_TILE], F32)
+            x_in_sb = out_pool.tile([P, N_TILE], F32, align_bytes=256)
             nc.scalar.copy(out=x_in_sb[:], in_=x_in[m][n][:])
             nc.sync.dma_start(out=out_0[b_rows, n_cols], in_=x_in_sb[:])
-            k1_sb = out_pool.tile([P, N_TILE], F32)
+            k1_sb = out_pool.tile([P, N_TILE], F32, align_bytes=256)
             nc.vector.tensor_tensor(out=k1_sb[:], in0=x_in_sb[:], in1=base[:, m, n_cols], op=ALU.add)
             nc.sync.dma_start(out=out_1[b_rows, n_cols], in_=k1_sb[:])
 

@@ -235,8 +235,17 @@ def tile_ltccell_pa_k_kernel(
 
         sort_words(0)
         flip(0)
+        spreads = []
+        for v, (spread, copy_out) in enumerate(((tau_sb, nc.scalar.copy), (bias_sb, nc.vector.tensor_copy))):
+            for n in range(COL_TILES):
+                n_cols = slice(n * N_TILE, (n + 1) * N_TILE)
+                repeated = work_pool.tile([P, N_TILE], F32, name="repeated%d%d" % (v, n), tag="work")
+                nc.tensor.matmul(out=repeated[:], lhsT=ones[:], rhs=vec_rows[:, v, n_cols], start=True, stop=True)
+                spreads.append((copy_out, spread[:, n_cols], repeated))
         quantize(0, 0, 2)
         quantize(0, 2, 2)
+        for copy_out, target, repeated in spreads:
+            copy_out(out=target, in_=repeated[:])
         sort_words(1)
 
         pre = new_banks("pre")
@@ -249,13 +258,6 @@ def tile_ltccell_pa_k_kernel(
                 quantize(next_chunk, 0, raw_tiles[next_chunk].shape[2] // K_PASS)
                 if next_chunk + 1 < A_CHUNKS:
                     sort_words(next_chunk + 1)
-
-        for v, (spread, copy_out) in enumerate(((tau_sb, nc.scalar.copy), (bias_sb, nc.vector.tensor_copy))):
-            for n in range(COL_TILES):
-                n_cols = slice(n * N_TILE, (n + 1) * N_TILE)
-                repeated = work_pool.tile([P, N_TILE], F32, tag="work")
-                nc.tensor.matmul(out=repeated[:], lhsT=ones[:], rhs=vec_rows[:, v, n_cols], start=True, stop=True)
-                copy_out(out=spread[:, n_cols], in_=repeated[:])
 
         for g in range(X_GROUPS, A_GROUPS):
             mx_passes(pre, GATE_SLOT + g, g, start=False, stop=(g == A_GROUPS - 1))

@@ -313,15 +313,16 @@ def tile_ltccell_pa_k_kernel(
             )
             nc.vector.tensor_tensor(out=base[:, m, n_cols], in0=base[:, m, n_cols], in1=gated[:], op=ALU.add)
 
-        def write_out(m, n):
-            b_rows = slice(m * P, (m + 1) * P)
+        def write_out(n):
             n_cols = slice(n * N_TILE, (n + 1) * N_TILE)
-            x_in_sb = out_pool.tile([P, N_TILE], F32, align_bytes=256)
-            nc.scalar.copy(out=x_in_sb[:], in_=x_in[m][n][:])
-            nc.sync.dma_start(out=out_0[b_rows, n_cols], in_=x_in_sb[:])
-            k1_sb = out_pool.tile([P, N_TILE], F32, align_bytes=256)
-            nc.vector.tensor_tensor(out=k1_sb[:], in0=x_in_sb[:], in1=base[:, m, n_cols], op=ALU.add)
-            nc.sync.dma_start(out=out_1[b_rows, n_cols], in_=k1_sb[:])
+            for m in range(ROW_TILES):
+                x_in_sb = out_pool.tile([P, N_TILE], F32, align_bytes=256)
+                nc.scalar.copy(out=x_in_sb[:], in_=x_in[m][n][:])
+                nc.scalar.dma_start(out=out_0[m * P : (m + 1) * P, n_cols], in_=x_in_sb[:])
+                other = ROW_TILES - 1 - m
+                k1_sb = out_pool.tile([P, N_TILE], F32, align_bytes=256)
+                nc.vector.tensor_tensor(out=k1_sb[:], in0=x_in[other][n][:], in1=base[:, other, n_cols], op=ALU.add)
+                nc.sync.dma_start(out=out_1[other * P : (other + 1) * P, n_cols], in_=k1_sb[:])
 
         x_in = new_banks("x_in")
         for piece in range(IN_SLOT, len(pieces)):
@@ -331,5 +332,4 @@ def tile_ltccell_pa_k_kernel(
             fetch(piece + W_BUFS)
             if g == X_GROUPS - 1:
                 for n in range(first_n, first_n + count):
-                    for m in range(ROW_TILES):
-                        write_out(m, n)
+                    write_out(n)

from contextlib import ExitStack

import concourse.mybir as mybir
from concourse.masks import make_identity

F32 = mybir.dt.float32
BF16 = mybir.dt.bfloat16
I32 = mybir.dt.int32
U32 = mybir.dt.uint32
U8 = mybir.dt.uint8
FP8X4 = mybir.dt.float8_e4m3fn_x4
ALU = mybir.AluOpType
ACT = mybir.ActivationFunctionType

P = 128
PACK = 4
K_PASS = P * PACK
B, IN, H = 256, 8192, 1024
ROW_TILES = B // P
N_TILE = 512
COL_TILES = H // N_TILE
X_GROUPS = IN // K_PASS
H_GROUPS = H // K_PASS
A_GROUPS = X_GROUPS + H_GROUPS
CHUNK_GROUPS = 4
X_CHUNKS = X_GROUPS // CHUNK_GROUPS
A_CHUNKS = X_CHUNKS + 1
CHUNKS_AHEAD = 2
PLANES_PER_BLOCK = 4
QUADRANTS = 4
W_BUFS = 12
TAPER_GROUPS = 4

FLOPS = 2 * B * H * (IN + (IN + H) + H)


def tile_ltccell_pa_k_kernel(
    tc,
    x,
    h,
    tau,
    W_in_words,
    W_in_scales,
    W_rec_words,
    W_rec_scales,
    gate_w_words,
    gate_w_scales,
    gate_b,
    out_0,
    out_1,
):
    nc = tc.nc

    GATE_SLOT = 0
    REC_SLOT = GATE_SLOT + A_GROUPS
    IN_SLOT = REC_SLOT + H_GROUPS
    N_SLOTS = IN_SLOT + X_GROUPS
    slot_words = []
    scales_at = {}
    for first_slot, words, scales in (
        (GATE_SLOT, gate_w_words, gate_w_scales),
        (REC_SLOT, W_rec_words, W_rec_scales),
        (IN_SLOT, W_in_words, W_in_scales),
    ):
        groups = words.shape[0]
        scales_at[first_slot] = (scales, groups)
        for g in range(groups):
            slot_words.append(words[g].rearrange("p n t -> p (n t)").bitcast(I32))
    N_BLOCKS = N_SLOTS // PLANES_PER_BLOCK
    pieces = [(slot, 0, COL_TILES) for slot in range(N_SLOTS - TAPER_GROUPS)]
    for n in range(COL_TILES):
        pieces.extend([(slot, n, 1) for slot in range(N_SLOTS - TAPER_GROUPS, N_SLOTS)])

    with ExitStack() as ctx:
        keep = ctx.enter_context(tc.tile_pool(name="keep", bufs=1))
        raw_pool = ctx.enter_context(tc.tile_pool(name="raw", bufs=X_CHUNKS))
        ordered_pool = ctx.enter_context(tc.tile_pool(name="ordered", bufs=2))
        grouped_pool = ctx.enter_context(tc.tile_pool(name="grouped", bufs=2))
        w_pool = ctx.enter_context(tc.tile_pool(name="w", bufs=W_BUFS))
        gate_pool = ctx.enter_context(tc.tile_pool(name="gate", bufs=2))
        out_pool = ctx.enter_context(tc.tile_pool(name="out", bufs=ROW_TILES * COL_TILES))
        acc_pool = ctx.enter_context(tc.psum_pool(name="acc", bufs=1))
        work_pool = ctx.enter_context(tc.psum_pool(name="work", bufs=CHUNK_GROUPS))
        ctx.enter_context(tc.manual_schedule())

        a_codes = keep.tile([P, A_GROUPS, B], U32, align_bytes=64)
        a_planes = keep.tile([P, A_GROUPS, B], U8, align_bytes=64)
        w_planes = keep.tile([P, N_BLOCKS, H], U8, align_bytes=256)
        h_raw = keep.tile([P, ROW_TILES, H], BF16, align_bytes=256)
        identity = keep.tile([P, P], F32)
        ones = keep.tile([P, P], BF16)
        vec_rows = keep.tile([P, 2, H], BF16)
        tau_sb = keep.tile([P, H], F32)
        bias_sb = keep.tile([P, H], F32)
        base = keep.tile([P, ROW_TILES, H], F32)
        half_rec = keep.tile([P, ROW_TILES, H], F32)

        warm = keep.tile([P, 2], F32)
        nc.vector.memset(warm[:, 0:1], 0.0)
        nc.scalar.copy(out=warm[:, 1:2], in_=warm[:, 0:1])
        nc.vector.memset(w_planes[:].rearrange("p c n -> p (c n)").bitcast(I32), 0)
        nc.vector.memset(vec_rows[:].rearrange("p v n -> p (v n)").bitcast(I32), 0)
        nc.vector.memset(ones[:], 1.0)
        make_identity(nc, identity[:])

        raw_tiles = {}
        w_tiles = {}

        def load_raw(chunk):
            if chunk < X_CHUNKS:
                raw = raw_pool.tile([P, ROW_TILES, CHUNK_GROUPS * K_PASS], BF16, align_bytes=256)
                k_cols = slice(chunk * CHUNK_GROUPS * K_PASS, (chunk + 1) * CHUNK_GROUPS * K_PASS)
                nc.sync.dma_start(out=raw[:], in_=x[:, k_cols].rearrange("(m p) k -> p m k", p=P))
                raw_tiles[chunk] = raw
            elif chunk < A_CHUNKS:
                nc.sync.dma_start(out=h_raw[:], in_=h.rearrange("(m p) k -> p m k", p=P))
                raw_tiles[chunk] = h_raw

        def plane_loads(first_slot):
            scales, groups = scales_at[first_slot]
            end_slot = first_slot + groups
            found = []
            for block in range(first_slot // PLANES_PER_BLOCK, (end_slot - 1) // PLANES_PER_BLOCK + 1):
                lo = max(first_slot, block * PLANES_PER_BLOCK)
                hi = min(end_slot, (block + 1) * PLANES_PER_BLOCK)
                for quad in range(QUADRANTS):
                    row = 32 * quad + 4 * (lo % PLANES_PER_BLOCK)
                    found.append(
                        (
                            w_planes[row : row + 4 * (hi - lo), block, :],
                            scales[lo - first_slot : hi - first_slot, 4 * quad : 4 * quad + 4, :],
                        )
                    )
            return found

        all_planes = plane_loads(GATE_SLOT) + plane_loads(REC_SLOT) + plane_loads(IN_SLOT)
        pool_planes = [pair for i, pair in enumerate(all_planes) if i % QUADRANTS < 2]
        sync_planes = [pair for i, pair in enumerate(all_planes) if i % QUADRANTS >= 2]

        woven = [0]

        def weave():
            if woven[0] < len(sync_planes):
                plane_out, plane_in = sync_planes[woven[0]]
                nc.sync.dma_start(out=plane_out.bitcast(I32), in_=plane_in.bitcast(I32))
                woven[0] += 1

        def fetch(piece):
            if piece < len(pieces):
                slot, first_n, count = pieces[piece]
                w = w_pool.tile([P, count * N_TILE], I32, align_bytes=256)
                nc.sync.dma_start(out=w[:], in_=slot_words[slot][:, first_n * N_TILE : (first_n + count) * N_TILE])
                w_tiles[piece] = w
                weave()

        ordered_tiles = {}
        grouped_tiles = {}

        def sort_words(chunk):
            raw = raw_tiles[chunk]
            groups = raw.shape[2] // K_PASS
            ordered = ordered_pool.tile([P, ROW_TILES, CHUNK_GROUPS, 2, P], F32)
            for m in range(ROW_TILES):
                copy_words = nc.vector.tensor_copy if m % 2 == 0 else nc.scalar.copy
                copy_words(
                    out=ordered[:, m, 0:groups, :, :],
                    in_=raw[:, m, :].bitcast(F32).rearrange("p (g q u) -> p g u q", q=P, u=2),
                )
            ordered_tiles[chunk] = ordered

        def flip(chunk):
            ordered = ordered_tiles[chunk]
            groups = raw_tiles[chunk].shape[2] // K_PASS
            grouped = grouped_pool.tile([P, CHUNK_GROUPS, B * PACK], BF16, align_bytes=64)
            for gi in range(groups):
                flipped = work_pool.tile([P, 2, B], F32, tag="work")
                for m in range(ROW_TILES):
                    for u in range(2):
                        nc.tensor.transpose(flipped[:, u, m * P : (m + 1) * P], ordered[:, m, gi, u, :], identity[:])
                copy_out = nc.vector.tensor_copy if gi % 2 == 0 else nc.scalar.copy
                copy_out(
                    out=grouped[:, gi, :].bitcast(F32).rearrange("p (b u) -> p b u", u=2),
                    in_=flipped[:].rearrange("p u b -> p b u"),
                )
            grouped_tiles[chunk] = grouped

        def quantize(chunk, first_gi, count):
            first = chunk * CHUNK_GROUPS + first_gi
            nc.vector.quantize_mx(
                out=a_codes[:, first : first + count, :].rearrange("p g b -> p (g b)").bitcast(FP8X4),
                scales=a_planes[:, first : first + count, :].rearrange("p g b -> p (g b)"),
                in_=grouped_tiles[chunk][:, first_gi : first_gi + count, :].rearrange("p g e -> p (g e)"),
            )

        def new_banks(label):
            return [
                [
                    acc_pool.tile([P, N_TILE], F32, name="%s%d%d" % (label, m, n), tag="acc%d%d" % (m, n))
                    for n in range(COL_TILES)
                ]
                for m in range(ROW_TILES)
            ]

        def mx_passes(banks, piece, a_group, start, stop):
            slot, first_n, count = pieces[piece]
            block = slot // PLANES_PER_BLOCK
            row = 4 * (slot % PLANES_PER_BLOCK)
            for m in range(ROW_TILES):
                b_cols = slice(m * P, (m + 1) * P)
                for i in range(count):
                    n = first_n + i
                    nc.tensor.matmul_mx(
                        out=banks[m][n][:],
                        lhsT=a_codes[:, a_group, b_cols].bitcast(FP8X4),
                        lhsT_scale=a_planes[:, a_group, b_cols],
                        rhs=w_tiles[piece][:, i * N_TILE : (i + 1) * N_TILE].bitcast(FP8X4),
                        rhs_scale=w_planes[row:P, block, n * N_TILE : (n + 1) * N_TILE],
                        start=start,
                        stop=stop,
                    )

        nc.scalar.dma_start(out=vec_rows[0:1, 0, :], in_=tau.unsqueeze(0))
        nc.scalar.dma_start(out=vec_rows[0:1, 1, :], in_=gate_b.unsqueeze(0))
        for plane_out, plane_in in pool_planes:
            nc.gpsimd.dma_start(out=plane_out.bitcast(F32), in_=plane_in.bitcast(F32))
        for chunk in range(A_CHUNKS):
            load_raw(chunk)
            if chunk == 0:
                weave()
                weave()
            fetch(2 * chunk)
            fetch(2 * chunk + 1)
        for slot in range(2 * A_CHUNKS, W_BUFS):
            fetch(slot)

        sort_words(0)
        flip(0)
        spreads = []
        for v, (spread, copy_out) in enumerate(((tau_sb, nc.scalar.copy), (bias_sb, nc.vector.tensor_copy))):
            for n in range(COL_TILES):
                n_cols = slice(n * N_TILE, (n + 1) * N_TILE)
                repeated = work_pool.tile([P, N_TILE], F32, name="repeated%d%d" % (v, n), tag="work")
                nc.tensor.matmul(out=repeated[:], lhsT=ones[:], rhs=vec_rows[:, v, n_cols], start=True, stop=True)
                spreads.append((copy_out, spread[:, n_cols], repeated))
        quantize(0, 0, 2)
        quantize(0, 2, 2)
        for copy_out, target, repeated in spreads:
            copy_out(out=target, in_=repeated[:])
        sort_words(1)

        pre = new_banks("pre")
        for g in range(X_GROUPS):
            mx_passes(pre, GATE_SLOT + g, g, start=(g == 0), stop=False)
            fetch(GATE_SLOT + g + W_BUFS)
            next_chunk = (g + 1) // 2
            if g % 2 == 1 and next_chunk < A_CHUNKS:
                flip(next_chunk)
                quantize(next_chunk, 0, raw_tiles[next_chunk].shape[2] // K_PASS)
                if next_chunk + 1 < A_CHUNKS:
                    sort_words(next_chunk + 1)

        for g in range(X_GROUPS, A_GROUPS):
            mx_passes(pre, GATE_SLOT + g, g, start=False, stop=(g == A_GROUPS - 1))
            fetch(GATE_SLOT + g + W_BUFS)

        soft = keep.tile([P, H], F32)
        nc.scalar.activation(out=soft[:], in_=tau_sb[:], func=ACT.Abs)
        nc.scalar.activation(out=soft[:], in_=soft[:], func=ACT.Exp, scale=-1.0)
        nc.scalar.activation(out=soft[:], in_=soft[:], func=ACT.Ln, bias=1.0)

        tiles = [(m, n) for m in range(ROW_TILES) for n in range(COL_TILES)]
        pre_b = {}
        for m, n in tiles:
            biased = gate_pool.tile([P, N_TILE], F32, bufs=len(tiles))
            nc.vector.tensor_tensor(
                out=biased[:], in0=pre[m][n][:], in1=bias_sb[:, n * N_TILE : (n + 1) * N_TILE], op=ALU.add
            )
            pre_b[(m, n)] = biased

        rec = [
            [work_pool.tile([P, N_TILE], F32, name="rec%d%d" % (m, n), tag="work") for n in range(COL_TILES)]
            for m in range(ROW_TILES)
        ]
        for g in range(H_GROUPS):
            mx_passes(rec, REC_SLOT + g, X_GROUPS + g, start=(g == 0), stop=(g == H_GROUPS - 1))
            fetch(REC_SLOT + g + W_BUFS)

        for m, n in tiles:
            n_cols = slice(n * N_TILE, (n + 1) * N_TILE)
            nc.scalar.activation(out=half_rec[:, m, n_cols], in_=rec[m][n][:], func=ACT.Copy, scale=0.5)

        softplus = keep.tile([P, H], F32)
        nc.vector.scalar_tensor_tensor(
            out=softplus[:], in0=tau_sb[:], scalar=0.0, in1=soft[:], op0=ALU.max, op1=ALU.add
        )
        inv_tau_p = keep.tile([P, H], F32)
        nc.scalar.activation(out=inv_tau_p[:], in_=softplus[:], func=ACT.Ln, bias=1.0)
        nc.scalar.activation(out=inv_tau_p[:], in_=inv_tau_p[:], func=ACT.Exp, scale=-1.0)
        for m in range(ROW_TILES):
            nc.vector.scalar_tensor_tensor(
                out=base[:, m, :], in0=h_raw[:, m, :], scalar=-1.0, in1=inv_tau_p[:], op0=ALU.mult, op1=ALU.mult
            )

        for m, n in tiles:
            n_cols = slice(n * N_TILE, (n + 1) * N_TILE)
            inner = gate_pool.tile([P, N_TILE], F32)
            nc.scalar.activation(out=inner[:], in_=pre_b[(m, n)][:], func=ACT.Tanh)
            outer = gate_pool.tile([P, N_TILE], F32)
            nc.scalar.activation(out=outer[:], in_=inner[:], func=ACT.Tanh, scale=0.5)
            gated = gate_pool.tile([P, N_TILE], F32)
            nc.vector.scalar_tensor_tensor(
                out=gated[:], in0=outer[:], scalar=1.0, in1=half_rec[:, m, n_cols], op0=ALU.add, op1=ALU.mult
            )
            nc.vector.tensor_tensor(out=base[:, m, n_cols], in0=base[:, m, n_cols], in1=gated[:], op=ALU.add)

        def write_out(n):
            n_cols = slice(n * N_TILE, (n + 1) * N_TILE)
            for m in range(ROW_TILES):
                x_in_sb = out_pool.tile([P, N_TILE], F32, align_bytes=256)
                nc.scalar.copy(out=x_in_sb[:], in_=x_in[m][n][:])
                nc.scalar.dma_start(out=out_0[m * P : (m + 1) * P, n_cols], in_=x_in_sb[:])
                other = ROW_TILES - 1 - m
                k1_sb = out_pool.tile([P, N_TILE], F32, align_bytes=256)
                nc.vector.tensor_tensor(out=k1_sb[:], in0=x_in[other][n][:], in1=base[:, other, n_cols], op=ALU.add)
                nc.sync.dma_start(out=out_1[other * P : (other + 1) * P, n_cols], in_=k1_sb[:])

        x_in = new_banks("x_in")
        for piece in range(IN_SLOT, len(pieces)):
            slot, first_n, count = pieces[piece]
            g = slot - IN_SLOT
            mx_passes(x_in, piece, g, start=(g == 0), stop=(g == X_GROUPS - 1))
            fetch(piece + W_BUFS)
            if g == X_GROUPS - 1:
                for n in range(first_n, first_n + count):
                    write_out(n)
